import numpy as np
import ml_dtypes

BF16 = ml_dtypes.bfloat16


def bf(x):
    return np.asarray(x, np.float32).astype(BF16)


def f32(x):
    return np.asarray(x, np.float32)


def f64(x):
    return np.asarray(x).astype(np.float64)


def striped(idx):
    return np.tile(idx.reshape(-1, 16).T, (8, 1))


P, C, S, K, BN, H2, H3, N = 2, 256, 512, 4, 512, 128, 128, 4096
B3 = 0.25


def relu(v):
    return np.maximum(v, 0.0)


def setup_inputs():
    return {
        "tables": f32(0.5 * np.random.standard_normal((P, C, S))),
        "w1": bf(np.random.standard_normal((P * C, H2)) * np.sqrt(2.0 / (P * C))),
        "b1": f32(0.1 * np.random.standard_normal((H2, 1))),
        "w2": bf(np.random.standard_normal((H2, H3)) * np.sqrt(2.0 / H2)),
        "b2": f32(0.1 * np.random.standard_normal((H3, 1))),
        "w3": bf(np.random.standard_normal((H3, 1)) * np.sqrt(2.0 / H3)),
        "offs": striped(np.concatenate([np.random.permutation(S) for _ in range(N // S)])),
    }


def reference(tables, w1, b1, w2, b2, w3, offs):
    idx = offs[:16].T.reshape(-1)
    pick = idx.reshape(P, K, BN)
    t = f64(tables)
    acc = np.stack([sum(t[p][:, pick[p, k]] for k in range(K)) for p in range(P)])
    x = relu(acc).reshape(P * C, BN)
    h1 = relu(f64(w1).T @ x + f64(b1))
    h2 = relu(f64(w2).T @ h1 + f64(b2))
    return (f64(w3) * h2).sum(axis=0, keepdims=True) + B3

@@ -1,0 +1,74 @@
+import concourse.mybir as mybir
+
+F32, BF16, U16 = mybir.dt.float32, mybir.dt.bfloat16, mybir.dt.uint16
+ADD = mybir.AluOpType.add
+RELU = mybir.ActivationFunctionType.Relu
+COPY = mybir.ActivationFunctionType.Copy
+
+SIDES, CHANNELS, FEATURES = 2, 256, 512
+SLOTS, POSITIONS = 4, 512
+HIDDEN = 128
+LIST = SIDES * SLOTS * POSITIONS
+P = 128
+BLOCKS = SIDES * CHANNELS // P
+RUN = POSITIONS // 16
+OUT_BIAS = 0.25
+
+FLOPS = 2 * POSITIONS * (SIDES * CHANNELS * HIDDEN + HIDDEN * HIDDEN + HIDDEN)
+
+
+def tile_halfkpnetwork_kernel(tc, tables, w1, b1, w2, b2, w3, offs, out):
+    nc = tc.nc
+    table_blocks = tables.rearrange("p (h c) s -> (p h) c s", c=P)
+
+    with (
+        tc.tile_pool(name="held", bufs=1) as held,
+        tc.tile_pool(name="sums", bufs=3) as sums,
+        tc.psum_pool(name="psum", bufs=1) as psum,
+    ):
+        offsets = held.tile([P, LIST // 16], U16, name="offsets")
+        nc.sync.dma_start(offsets[:], offs)
+        windows = []
+        for b in range(BLOCKS):
+            window = held.tile([P, FEATURES], F32, name=f"window{b}")
+            nc.sync.dma_start(window[:], table_blocks[b])
+            windows.append(window)
+        w1_sb = held.tile([P, BLOCKS, HIDDEN], BF16, name="w1_sb")
+        nc.sync.dma_start(w1_sb[:], w1.rearrange("(b q) m -> q b m", q=P))
+        b1_sb = held.tile([HIDDEN, 1], F32, name="b1_sb")
+        nc.sync.dma_start(b1_sb[:], b1)
+        w2_sb = held.tile([HIDDEN, HIDDEN], BF16, name="w2_sb")
+        nc.sync.dma_start(w2_sb[:], w2)
+        b2_sb = held.tile([HIDDEN, 1], F32, name="b2_sb")
+        nc.sync.dma_start(b2_sb[:], b2)
+        w3_sb = held.tile([HIDDEN, 1], BF16, name="w3_sb")
+        nc.sync.dma_start(w3_sb[:], w3)
+
+        h1_ps = psum.tile([HIDDEN, POSITIONS], F32, name="h1_ps")
+        acc = None
+        for b in range(BLOCKS):
+            side = b // 2
+            for k in range(SLOTS):
+                run = side * SLOTS + k
+                picked = windows[b][:].indirect(offsets[:, run * RUN : (run + 1) * RUN])
+                shorter = acc if k > 0 else None
+                acc = sums.tile([P, POSITIONS], F32, name="acc")
+                if k == 0:
+                    nc.vector.tensor_copy(acc[:], picked)
+                else:
+                    nc.vector.tensor_tensor(acc[:], picked, shorter[:], ADD)
+            x = held.tile([P, POSITIONS], BF16, name=f"x{b}")
+            nc.scalar.activation(x[:], acc[:], RELU)
+            nc.tensor.matmul(h1_ps[:], w1_sb[:, b, :], x[:], start=(b == 0), stop=(b == BLOCKS - 1))
+
+        h1 = held.tile([HIDDEN, POSITIONS], BF16, name="h1")
+        nc.scalar.activation(h1[:], h1_ps[:], RELU, bias=b1_sb[:])
+        h2_ps = psum.tile([HIDDEN, POSITIONS], F32, name="h2_ps")
+        nc.tensor.matmul(h2_ps[:], w2_sb[:], h1[:], start=True, stop=True)
+        h2 = held.tile([HIDDEN, POSITIONS], BF16, name="h2")
+        nc.scalar.activation(h2[:], h2_ps[:], RELU, bias=b2_sb[:])
+        score_ps = psum.tile([1, POSITIONS], F32, name="score_ps")
+        nc.tensor.matmul(score_ps[:], w3_sb[:], h2[:], start=True, stop=True)
+        score = held.tile([1, POSITIONS], F32, name="score")
+        nc.scalar.activation(score[:], score_ps[:], COPY, bias=OUT_BIAS)
+        nc.sync.dma_start(out, score[:])

@@ -10,7 +10,8 @@ SLOTS, POSITIONS = 4, 512
 HIDDEN = 128
 LIST = SIDES * SLOTS * POSITIONS
 P = 128
-BLOCKS = SIDES * CHANNELS // P
+HALVES = CHANNELS // P
+BLOCKS = SIDES * HALVES
 RUN = POSITIONS // 16
 OUT_BIAS = 0.25
 
@@ -45,21 +46,23 @@ def tile_halfkpnetwork_kernel(tc, tables, w1, b1, w2, b2, w3, offs, out):
         nc.sync.dma_start(w3_sb[:], w3)
 
         h1_ps = psum.tile([HIDDEN, POSITIONS], F32, name="h1_ps")
-        acc = None
-        for b in range(BLOCKS):
-            side = b // 2
+        for side in range(SIDES):
+            acc = [None] * HALVES
             for k in range(SLOTS):
                 run = side * SLOTS + k
-                picked = windows[b][:].indirect(offsets[:, run * RUN : (run + 1) * RUN])
-                shorter = acc if k > 0 else None
-                acc = sums.tile([P, POSITIONS], F32, name="acc")
-                if k == 0:
-                    nc.vector.tensor_copy(acc[:], picked)
-                else:
-                    nc.vector.tensor_tensor(acc[:], picked, shorter[:], ADD)
-            x = held.tile([P, POSITIONS], BF16, name=f"x{b}")
-            nc.scalar.activation(x[:], acc[:], RELU)
-            nc.tensor.matmul(h1_ps[:], w1_sb[:, b, :], x[:], start=(b == 0), stop=(b == BLOCKS - 1))
+                for h in range(HALVES):
+                    picked = windows[side * HALVES + h][:].indirect(offsets[:, run * RUN : (run + 1) * RUN])
+                    longer = sums.tile([P, POSITIONS], F32, name=f"acc{h}")
+                    if k == 0:
+                        nc.vector.tensor_copy(longer[:], picked)
+                    else:
+                        nc.vector.tensor_tensor(longer[:], picked, acc[h][:], ADD)
+                    acc[h] = longer
+            for h in range(HALVES):
+                b = side * HALVES + h
+                x = held.tile([P, POSITIONS], BF16, name=f"x{b}")
+                nc.scalar.activation(x[:], acc[h][:], RELU)
+                nc.tensor.matmul(h1_ps[:], w1_sb[:, b, :], x[:], start=(b == 0), stop=(b == BLOCKS - 1))
 
         h1 = held.tile([HIDDEN, POSITIONS], BF16, name="h1")
         nc.scalar.activation(h1[:], h1_ps[:], RELU, bias=b1_sb[:])

@@ -13,6 +13,9 @@ P = 128
 HALVES = CHANNELS // P
 BLOCKS = SIDES * HALVES
 RUN = POSITIONS // 16
+CHUNKS = 2
+WIDTH = POSITIONS // CHUNKS
+PIECE = WIDTH // 16
 OUT_BIAS = 0.25
 
 FLOPS = 2 * POSITIONS * (SIDES * CHANNELS * HIDDEN + HIDDEN * HIDDEN + HIDDEN)
@@ -25,7 +28,8 @@ def tile_halfkpnetwork_kernel(tc, tables, w1, b1, w2, b2, w3, offs, out):
     with (
         tc.tile_pool(name="held", bufs=1) as held,
         tc.tile_pool(name="sums", bufs=3) as sums,
-        tc.psum_pool(name="psum", bufs=1) as psum,
+        tc.tile_pool(name="work", bufs=2) as work,
+        tc.psum_pool(name="psum", bufs=2) as psum,
     ):
         offsets = held.tile([P, LIST // 16], U16, name="offsets")
         nc.sync.dma_start(offsets[:], offs)
@@ -45,33 +49,34 @@ def tile_halfkpnetwork_kernel(tc, tables, w1, b1, w2, b2, w3, offs, out):
         w3_sb = held.tile([HIDDEN, 1], BF16, name="w3_sb")
         nc.sync.dma_start(w3_sb[:], w3)
 
-        h1_ps = psum.tile([HIDDEN, POSITIONS], F32, name="h1_ps")
-        for side in range(SIDES):
-            acc = [None] * HALVES
-            for k in range(SLOTS):
-                run = side * SLOTS + k
+        for c in range(CHUNKS):
+            h1_ps = psum.tile([HIDDEN, WIDTH], F32, name="h1_ps")
+            for side in range(SIDES):
+                acc = [None] * HALVES
+                for k in range(SLOTS):
+                    first = (side * SLOTS + k) * RUN + c * PIECE
+                    for h in range(HALVES):
+                        picked = windows[side * HALVES + h][:].indirect(offsets[:, first : first + PIECE])
+                        longer = sums.tile([P, WIDTH], F32, name=f"acc{h}")
+                        if k == 0:
+                            nc.vector.tensor_copy(longer[:], picked)
+                        else:
+                            nc.vector.tensor_tensor(longer[:], picked, acc[h][:], ADD)
+                        acc[h] = longer
                 for h in range(HALVES):
-                    picked = windows[side * HALVES + h][:].indirect(offsets[:, run * RUN : (run + 1) * RUN])
-                    longer = sums.tile([P, POSITIONS], F32, name=f"acc{h}")
-                    if k == 0:
-                        nc.vector.tensor_copy(longer[:], picked)
-                    else:
-                        nc.vector.tensor_tensor(longer[:], picked, acc[h][:], ADD)
-                    acc[h] = longer
-            for h in range(HALVES):
-                b = side * HALVES + h
-                x = held.tile([P, POSITIONS], BF16, name=f"x{b}")
-                nc.scalar.activation(x[:], acc[h][:], RELU)
-                nc.tensor.matmul(h1_ps[:], w1_sb[:, b, :], x[:], start=(b == 0), stop=(b == BLOCKS - 1))
+                    b = side * HALVES + h
+                    x = work.tile([P, WIDTH], BF16, name=f"x{h}")
+                    nc.scalar.activation(x[:], acc[h][:], RELU)
+                    nc.tensor.matmul(h1_ps[:], w1_sb[:, b, :], x[:], start=(b == 0), stop=(b == BLOCKS - 1))
 
-        h1 = held.tile([HIDDEN, POSITIONS], BF16, name="h1")
-        nc.scalar.activation(h1[:], h1_ps[:], RELU, bias=b1_sb[:])
-        h2_ps = psum.tile([HIDDEN, POSITIONS], F32, name="h2_ps")
-        nc.tensor.matmul(h2_ps[:], w2_sb[:], h1[:], start=True, stop=True)
-        h2 = held.tile([HIDDEN, POSITIONS], BF16, name="h2")
-        nc.scalar.activation(h2[:], h2_ps[:], RELU, bias=b2_sb[:])
-        score_ps = psum.tile([1, POSITIONS], F32, name="score_ps")
-        nc.tensor.matmul(score_ps[:], w3_sb[:], h2[:], start=True, stop=True)
-        score = held.tile([1, POSITIONS], F32, name="score")
-        nc.scalar.activation(score[:], score_ps[:], COPY, bias=OUT_BIAS)
-        nc.sync.dma_start(out, score[:])
+            h1 = work.tile([HIDDEN, WIDTH], BF16, name="h1")
+            nc.scalar.activation(h1[:], h1_ps[:], RELU, bias=b1_sb[:])
+            h2_ps = psum.tile([HIDDEN, WIDTH], F32, name="h2_ps")
+            nc.tensor.matmul(h2_ps[:], w2_sb[:], h1[:], start=True, stop=True)
+            h2 = work.tile([HIDDEN, WIDTH], BF16, name="h2")
+            nc.scalar.activation(h2[:], h2_ps[:], RELU, bias=b2_sb[:])
+            score_ps = psum.tile([1, WIDTH], F32, name="score_ps")
+            nc.tensor.matmul(score_ps[:], w3_sb[:], h2[:], start=True, stop=True)
+            score = work.tile([1, WIDTH], F32, name="score")
+            nc.scalar.activation(score[:], score_ps[:], COPY, bias=OUT_BIAS)
+            nc.sync.dma_start(out[:, c * WIDTH : (c + 1) * WIDTH], score[:])

@@ -27,7 +27,8 @@ def tile_halfkpnetwork_kernel(tc, tables, w1, b1, w2, b2, w3, offs, out):
 
     with (
         tc.tile_pool(name="held", bufs=1) as held,
-        tc.tile_pool(name="sums", bufs=3) as sums,
+        tc.tile_pool(name="sums", bufs=2) as sums,
+        tc.tile_pool(name="bags", bufs=2 * BLOCKS) as bags,
         tc.tile_pool(name="work", bufs=2) as work,
         tc.psum_pool(name="psum", bufs=2) as psum,
     ):
@@ -49,26 +50,28 @@ def tile_halfkpnetwork_kernel(tc, tables, w1, b1, w2, b2, w3, offs, out):
         w3_sb = held.tile([HIDDEN, 1], BF16, name="w3_sb")
         nc.sync.dma_start(w3_sb[:], w3)
 
+        acc = [None] * BLOCKS
+        for k in range(SLOTS - 1):
+            for b in range(BLOCKS):
+                run = (b // HALVES) * SLOTS + k
+                picked = windows[b][:].indirect(offsets[:, run * RUN : (run + 1) * RUN])
+                longer = sums.tile([P, POSITIONS], F32, name=f"acc{b}")
+                if k == 0:
+                    nc.vector.tensor_copy(longer[:], picked)
+                else:
+                    nc.vector.tensor_tensor(longer[:], picked, acc[b][:], ADD)
+                acc[b] = longer
+
         for c in range(CHUNKS):
             h1_ps = psum.tile([HIDDEN, WIDTH], F32, name="h1_ps")
-            for side in range(SIDES):
-                acc = [None] * HALVES
-                for k in range(SLOTS):
-                    first = (side * SLOTS + k) * RUN + c * PIECE
-                    for h in range(HALVES):
-                        picked = windows[side * HALVES + h][:].indirect(offsets[:, first : first + PIECE])
-                        longer = sums.tile([P, WIDTH], F32, name=f"acc{h}")
-                        if k == 0:
-                            nc.vector.tensor_copy(longer[:], picked)
-                        else:
-                            nc.vector.tensor_tensor(longer[:], picked, acc[h][:], ADD)
-                        acc[h] = longer
-                for h in range(HALVES):
-                    b = side * HALVES + h
-                    x = work.tile([P, WIDTH], BF16, name=f"x{h}")
-                    nc.scalar.activation(x[:], acc[h][:], RELU)
-                    nc.tensor.matmul(h1_ps[:], w1_sb[:, b, :], x[:], start=(b == 0), stop=(b == BLOCKS - 1))
-
+            for b in range(BLOCKS):
+                first = ((b // HALVES) * SLOTS + SLOTS - 1) * RUN + c * PIECE
+                picked = windows[b][:].indirect(offsets[:, first : first + PIECE])
+                bag = bags.tile([P, WIDTH], F32, name="bag")
+                nc.vector.tensor_tensor(bag[:], picked, acc[b][:, c * WIDTH : (c + 1) * WIDTH], ADD)
+                x = bags.tile([P, WIDTH], BF16, name="x")
+                nc.scalar.activation(x[:], bag[:], RELU)
+                nc.tensor.matmul(h1_ps[:], w1_sb[:, b, :], x[:], start=(b == 0), stop=(b == BLOCKS - 1))
             h1 = work.tile([HIDDEN, WIDTH], BF16, name="h1")
             nc.scalar.activation(h1[:], h1_ps[:], RELU, bias=b1_sb[:])
             h2_ps = psum.tile([HIDDEN, WIDTH], F32, name="h2_ps")

@@ -16,6 +16,8 @@ RUN = POSITIONS // 16
 CHUNKS = 2
 WIDTH = POSITIONS // CHUNKS
 PIECE = WIDTH // 16
+LANES = 2
+LANE = WIDTH // LANES
 OUT_BIAS = 0.25
 
 FLOPS = 2 * POSITIONS * (SIDES * CHANNELS * HIDDEN + HIDDEN * HIDDEN + HIDDEN)
@@ -30,7 +32,7 @@ def tile_halfkpnetwork_kernel(tc, tables, w1, b1, w2, b2, w3, offs, out):
         tc.tile_pool(name="sums", bufs=2) as sums,
         tc.tile_pool(name="bags", bufs=2 * BLOCKS) as bags,
         tc.tile_pool(name="work", bufs=2) as work,
-        tc.psum_pool(name="psum", bufs=2) as psum,
+        tc.psum_pool(name="psum", bufs=1) as psum,
     ):
         offsets = held.tile([P, LIST // 16], U16, name="offsets")
         nc.sync.dma_start(offsets[:], offs)
@@ -63,7 +65,7 @@ def tile_halfkpnetwork_kernel(tc, tables, w1, b1, w2, b2, w3, offs, out):
                 acc[b] = longer
 
         for c in range(CHUNKS):
-            h1_ps = psum.tile([HIDDEN, WIDTH], F32, name="h1_ps")
+            h1_ps = [psum.tile([HIDDEN, LANE], F32, name=f"h1_ps{lane}") for lane in range(LANES)]
             for b in range(BLOCKS):
                 first = ((b // HALVES) * SLOTS + SLOTS - 1) * RUN + c * PIECE
                 picked = windows[b][:].indirect(offsets[:, first : first + PIECE])
@@ -71,15 +73,25 @@ def tile_halfkpnetwork_kernel(tc, tables, w1, b1, w2, b2, w3, offs, out):
                 nc.vector.tensor_tensor(bag[:], picked, acc[b][:, c * WIDTH : (c + 1) * WIDTH], ADD)
                 x = bags.tile([P, WIDTH], BF16, name="x")
                 nc.scalar.activation(x[:], bag[:], RELU)
-                nc.tensor.matmul(h1_ps[:], w1_sb[:, b, :], x[:], start=(b == 0), stop=(b == BLOCKS - 1))
-            h1 = work.tile([HIDDEN, WIDTH], BF16, name="h1")
-            nc.scalar.activation(h1[:], h1_ps[:], RELU, bias=b1_sb[:])
-            h2_ps = psum.tile([HIDDEN, WIDTH], F32, name="h2_ps")
-            nc.tensor.matmul(h2_ps[:], w2_sb[:], h1[:], start=True, stop=True)
-            h2 = work.tile([HIDDEN, WIDTH], BF16, name="h2")
-            nc.scalar.activation(h2[:], h2_ps[:], RELU, bias=b2_sb[:])
-            score_ps = psum.tile([1, WIDTH], F32, name="score_ps")
-            nc.tensor.matmul(score_ps[:], w3_sb[:], h2[:], start=True, stop=True)
+                for lane in range(LANES):
+                    nc.tensor.matmul(
+                        h1_ps[lane][:],
+                        w1_sb[:, b, :],
+                        x[:, lane * LANE : (lane + 1) * LANE],
+                        start=(b == 0),
+                        stop=(b == BLOCKS - 1),
+                    )
+            h1 = [work.tile([HIDDEN, LANE], BF16, name=f"h1_{lane}") for lane in range(LANES)]
+            h2_ps = [psum.tile([HIDDEN, LANE], F32, name=f"h2_ps{lane}") for lane in range(LANES)]
+            for lane in range(LANES):
+                nc.scalar.activation(h1[lane][:], h1_ps[lane][:], RELU, bias=b1_sb[:])
+                nc.tensor.matmul(h2_ps[lane][:], w2_sb[:], h1[lane][:], start=True, stop=True)
+            h2 = [work.tile([HIDDEN, LANE], BF16, name=f"h2_{lane}") for lane in range(LANES)]
+            score_ps = [psum.tile([1, LANE], F32, name=f"score_ps{lane}") for lane in range(LANES)]
+            for lane in range(LANES):
+                nc.scalar.activation(h2[lane][:], h2_ps[lane][:], RELU, bias=b2_sb[:])
+                nc.tensor.matmul(score_ps[lane][:], w3_sb[:], h2[lane][:], start=True, stop=True)
             score = work.tile([1, WIDTH], F32, name="score")
-            nc.scalar.activation(score[:], score_ps[:], COPY, bias=OUT_BIAS)
+            for lane in range(LANES):
+                nc.scalar.activation(score[:, lane * LANE : (lane + 1) * LANE], score_ps[lane][:], COPY, bias=OUT_BIAS)
             nc.sync.dma_start(out[:, c * WIDTH : (c + 1) * WIDTH], score[:])

@@ -56,12 +56,17 @@ def tile_halfkpnetwork_kernel(tc, tables, w1, b1, w2, b2, w3, offs, out):
         for k in range(SLOTS - 1):
             for b in range(BLOCKS):
                 run = (b // HALVES) * SLOTS + k
-                picked = windows[b][:].indirect(offsets[:, run * RUN : (run + 1) * RUN])
                 longer = sums.tile([P, POSITIONS], F32, name=f"acc{b}")
-                if k == 0:
-                    nc.vector.tensor_copy(longer[:], picked)
-                else:
-                    nc.vector.tensor_tensor(longer[:], picked, acc[b][:], ADD)
+                pieces = 2 if b == 0 and k < 2 else 1
+                width = POSITIONS // pieces
+                for i in range(pieces):
+                    first = run * RUN + i * width // 16
+                    picked = windows[b][:].indirect(offsets[:, first : first + width // 16])
+                    part = slice(i * width, (i + 1) * width)
+                    if k == 0:
+                        nc.vector.tensor_copy(longer[:, part], picked)
+                    else:
+                        nc.vector.tensor_tensor(longer[:, part], picked, acc[b][:, part], ADD)
                 acc[b] = longer
 
         for c in range(CHUNKS):

@@ -1,7 +1,7 @@
 import concourse.mybir as mybir
 
 F32, BF16, U16 = mybir.dt.float32, mybir.dt.bfloat16, mybir.dt.uint16
-ADD = mybir.AluOpType.add
+ADD, MAX = mybir.AluOpType.add, mybir.AluOpType.max
 RELU = mybir.ActivationFunctionType.Relu
 COPY = mybir.ActivationFunctionType.Copy
 
@@ -13,11 +13,8 @@ P = 128
 HALVES = CHANNELS // P
 BLOCKS = SIDES * HALVES
 RUN = POSITIONS // 16
-CHUNKS = 2
-WIDTH = POSITIONS // CHUNKS
-PIECE = WIDTH // 16
-LANES = 2
-LANE = WIDTH // LANES
+NARROW = 128
+CHUNK_LANES = ((192, 192), (NARROW,))
 OUT_BIAS = 0.25
 
 FLOPS = 2 * POSITIONS * (SIDES * CHANNELS * HIDDEN + HIDDEN * HIDDEN + HIDDEN)
@@ -30,9 +27,9 @@ def tile_halfkpnetwork_kernel(tc, tables, w1, b1, w2, b2, w3, offs, out):
     with (
         tc.tile_pool(name="held", bufs=1) as held,
         tc.tile_pool(name="sums", bufs=2) as sums,
-        tc.tile_pool(name="bags", bufs=2 * BLOCKS) as bags,
-        tc.tile_pool(name="work", bufs=2) as work,
+        tc.tile_pool(name="work", bufs=1) as work,
         tc.psum_pool(name="psum", bufs=1) as psum,
+        tc.psum_pool(name="narrow_psum", bufs=2) as narrow_psum,
     ):
         offsets = held.tile([P, LIST // 16], U16, name="offsets")
         nc.sync.dma_start(offsets[:], offs)
@@ -69,34 +66,56 @@ def tile_halfkpnetwork_kernel(tc, tables, w1, b1, w2, b2, w3, offs, out):
                         nc.vector.tensor_tensor(longer[:, part], picked, acc[b][:, part], ADD)
                 acc[b] = longer
 
-        for c in range(CHUNKS):
-            h1_ps = [psum.tile([HIDDEN, LANE], F32, name=f"h1_ps{lane}") for lane in range(LANES)]
+        def relu_on_scalar(to, of, bias=None):
+            nc.scalar.activation(to, of, RELU, bias=0.0 if bias is None else bias[:])
+
+        def relu_on_vector(to, of, bias=None):
+            if bias is None:
+                nc.vector.tensor_scalar_max(to, of, 0.0)
+            else:
+                nc.vector.tensor_scalar(to, of, bias[:], 0.0, ADD, MAX)
+
+        score = held.tile([1, POSITIONS], F32, name="score")
+        at = 0
+        for c, lanes in enumerate(CHUNK_LANES):
+            narrow = c == len(CHUNK_LANES) - 1
+            width = sum(lanes)
+            relu = relu_on_vector if narrow else relu_on_scalar
+            spans = [slice(sum(lanes[:i]), sum(lanes[: i + 1])) for i in range(len(lanes))]
+
+            def product(name, i, rows):
+                if narrow:
+                    return narrow_psum.tile([rows, lanes[i]], F32, name=f"narrow_{name}", tag="narrow")
+                return psum.tile([rows, lanes[i]], F32, name=f"{name}{i}")
+
+            h1_ps = [product("h1_ps", i, HIDDEN) for i in range(len(lanes))]
             for b in range(BLOCKS):
-                first = ((b // HALVES) * SLOTS + SLOTS - 1) * RUN + c * PIECE
-                picked = windows[b][:].indirect(offsets[:, first : first + PIECE])
-                bag = bags.tile([P, WIDTH], F32, name="bag")
-                nc.vector.tensor_tensor(bag[:], picked, acc[b][:, c * WIDTH : (c + 1) * WIDTH], ADD)
-                x = bags.tile([P, WIDTH], BF16, name="x")
-                nc.scalar.activation(x[:], bag[:], RELU)
-                for lane in range(LANES):
-                    nc.tensor.matmul(
-                        h1_ps[lane][:],
-                        w1_sb[:, b, :],
-                        x[:, lane * LANE : (lane + 1) * LANE],
-                        start=(b == 0),
-                        stop=(b == BLOCKS - 1),
-                    )
-            h1 = [work.tile([HIDDEN, LANE], BF16, name=f"h1_{lane}") for lane in range(LANES)]
-            h2_ps = [psum.tile([HIDDEN, LANE], F32, name=f"h2_ps{lane}") for lane in range(LANES)]
-            for lane in range(LANES):
-                nc.scalar.activation(h1[lane][:], h1_ps[lane][:], RELU, bias=b1_sb[:])
-                nc.tensor.matmul(h2_ps[lane][:], w2_sb[:], h1[lane][:], start=True, stop=True)
-            h2 = [work.tile([HIDDEN, LANE], BF16, name=f"h2_{lane}") for lane in range(LANES)]
-            score_ps = [psum.tile([1, LANE], F32, name=f"score_ps{lane}") for lane in range(LANES)]
-            for lane in range(LANES):
-                nc.scalar.activation(h2[lane][:], h2_ps[lane][:], RELU, bias=b2_sb[:])
-                nc.tensor.matmul(score_ps[lane][:], w3_sb[:], h2[lane][:], start=True, stop=True)
-            score = work.tile([1, WIDTH], F32, name="score")
-            for lane in range(LANES):
-                nc.scalar.activation(score[:, lane * LANE : (lane + 1) * LANE], score_ps[lane][:], COPY, bias=OUT_BIAS)
-            nc.sync.dma_start(out[:, c * WIDTH : (c + 1) * WIDTH], score[:])
+                first = (((b // HALVES) * SLOTS + SLOTS - 1) * POSITIONS + at) // 16
+                picked = windows[b][:].indirect(offsets[:, first : first + width // 16])
+                bag = work.tile([P, width], F32, name=f"bag{c}{b}")
+                nc.vector.tensor_tensor(bag[:], picked, acc[b][:, at : at + width], ADD)
+                x = work.tile([P, width], BF16, name=f"x{c}{b}")
+                if b == BLOCKS - 1:
+                    relu(x[:], bag[:])
+                else:
+                    relu_on_scalar(x[:], bag[:])
+                for i, span in enumerate(spans):
+                    nc.tensor.matmul(h1_ps[i][:], w1_sb[:, b, :], x[:, span], start=(b == 0), stop=(b == BLOCKS - 1))
+            h1 = work.tile([HIDDEN, width], BF16, name=f"h1{c}")
+            h2_ps = [product("h2_ps", i, HIDDEN) for i in range(len(lanes))]
+            for i, span in enumerate(spans):
+                relu(h1[:, span], h1_ps[i][:], b1_sb)
+                nc.tensor.matmul(h2_ps[i][:], w2_sb[:], h1[:, span], start=True, stop=True)
+            h2 = work.tile([HIDDEN, width], BF16, name=f"h2{c}")
+            score_ps = [product("score_ps", i, 1) for i in range(len(lanes))]
+            for i, span in enumerate(spans):
+                relu(h2[:, span], h2_ps[i][:], b2_sb)
+                nc.tensor.matmul(score_ps[i][:], w3_sb[:], h2[:, span], start=True, stop=True)
+            for i, span in enumerate(spans):
+                to = score[:, at + span.start : at + span.stop]
+                if narrow:
+                    nc.vector.tensor_scalar_add(to, score_ps[i][:], OUT_BIAS)
+                else:
+                    nc.scalar.activation(to, score_ps[i][:], COPY, bias=OUT_BIAS)
+            at += width
+        nc.sync.dma_start(out, score[:])

@@ -13,8 +13,8 @@ P = 128
 HALVES = CHANNELS // P
 BLOCKS = SIDES * HALVES
 RUN = POSITIONS // 16
-NARROW = 128
-CHUNK_LANES = ((192, 192), (NARROW,))
+NARROW = 96
+CHUNK_LANES = ((160, 128, 128), (NARROW,))
 OUT_BIAS = 0.25
 
 FLOPS = 2 * POSITIONS * (SIDES * CHANNELS * HIDDEN + HIDDEN * HIDDEN + HIDDEN)
@@ -28,8 +28,7 @@ def tile_halfkpnetwork_kernel(tc, tables, w1, b1, w2, b2, w3, offs, out):
         tc.tile_pool(name="held", bufs=1) as held,
         tc.tile_pool(name="sums", bufs=2) as sums,
         tc.tile_pool(name="work", bufs=1) as work,
-        tc.psum_pool(name="psum", bufs=1) as psum,
-        tc.psum_pool(name="narrow_psum", bufs=2) as narrow_psum,
+        tc.psum_pool(name="psum", bufs=2) as psum,
     ):
         offsets = held.tile([P, LIST // 16], U16, name="offsets")
         nc.sync.dma_start(offsets[:], offs)
@@ -84,9 +83,7 @@ def tile_halfkpnetwork_kernel(tc, tables, w1, b1, w2, b2, w3, offs, out):
             spans = [slice(sum(lanes[:i]), sum(lanes[: i + 1])) for i in range(len(lanes))]
 
             def product(name, i, rows):
-                if narrow:
-                    return narrow_psum.tile([rows, lanes[i]], F32, name=f"narrow_{name}", tag="narrow")
-                return psum.tile([rows, lanes[i]], F32, name=f"{name}{i}")
+                return psum.tile([rows, lanes[i]], F32, name=f"{name}{c}{i}", tag=f"lane{c}{i}")
 
             h1_ps = [product("h1_ps", i, HIDDEN) for i in range(len(lanes))]
             for b in range(BLOCKS):

@@ -92,11 +92,11 @@ def tile_halfkpnetwork_kernel(tc, tables, w1, b1, w2, b2, w3, offs, out):
                 bag = work.tile([P, width], F32, name=f"bag{c}{b}")
                 nc.vector.tensor_tensor(bag[:], picked, acc[b][:, at : at + width], ADD)
                 x = work.tile([P, width], BF16, name=f"x{c}{b}")
-                if b == BLOCKS - 1:
-                    relu(x[:], bag[:])
-                else:
+                if b < BLOCKS - 1:
                     relu_on_scalar(x[:], bag[:])
                 for i, span in enumerate(spans):
+                    if b == BLOCKS - 1:
+                        relu(x[:, span], bag[:, span])
                     nc.tensor.matmul(h1_ps[i][:], w1_sb[:, b, :], x[:, span], start=(b == 0), stop=(b == BLOCKS - 1))
             h1 = work.tile([HIDDEN, width], BF16, name=f"h1{c}")
             h2_ps = [product("h2_ps", i, HIDDEN) for i in range(len(lanes))]

@@ -68,18 +68,15 @@ def tile_halfkpnetwork_kernel(tc, tables, w1, b1, w2, b2, w3, offs, out):
         def relu_on_scalar(to, of, bias=None):
             nc.scalar.activation(to, of, RELU, bias=0.0 if bias is None else bias[:])
 
-        def relu_on_vector(to, of, bias=None):
-            if bias is None:
-                nc.vector.tensor_scalar_max(to, of, 0.0)
-            else:
-                nc.vector.tensor_scalar(to, of, bias[:], 0.0, ADD, MAX)
+        def relu_on_vector(to, of, bias):
+            nc.vector.tensor_scalar(to, of, bias[:], 0.0, ADD, MAX)
 
         score = held.tile([1, POSITIONS], F32, name="score")
         at = 0
         for c, lanes in enumerate(CHUNK_LANES):
             narrow = c == len(CHUNK_LANES) - 1
             width = sum(lanes)
-            relu = relu_on_vector if narrow else relu_on_scalar
+            mlp_relu = relu_on_scalar if narrow else relu_on_vector
             spans = [slice(sum(lanes[:i]), sum(lanes[: i + 1])) for i in range(len(lanes))]
 
             def product(name, i, rows):
@@ -92,27 +89,27 @@ def tile_halfkpnetwork_kernel(tc, tables, w1, b1, w2, b2, w3, offs, out):
                 bag = work.tile([P, width], F32, name=f"bag{c}{b}")
                 nc.vector.tensor_tensor(bag[:], picked, acc[b][:, at : at + width], ADD)
                 x = work.tile([P, width], BF16, name=f"x{c}{b}")
-                if b < BLOCKS - 1:
+                if b < BLOCKS - 1 or narrow:
                     relu_on_scalar(x[:], bag[:])
                 for i, span in enumerate(spans):
-                    if b == BLOCKS - 1:
-                        relu(x[:, span], bag[:, span])
+                    if b == BLOCKS - 1 and not narrow:
+                        relu_on_scalar(x[:, span], bag[:, span])
                     nc.tensor.matmul(h1_ps[i][:], w1_sb[:, b, :], x[:, span], start=(b == 0), stop=(b == BLOCKS - 1))
             h1 = work.tile([HIDDEN, width], BF16, name=f"h1{c}")
             h2_ps = [product("h2_ps", i, HIDDEN) for i in range(len(lanes))]
             for i, span in enumerate(spans):
-                relu(h1[:, span], h1_ps[i][:], b1_sb)
+                mlp_relu(h1[:, span], h1_ps[i][:], b1_sb)
                 nc.tensor.matmul(h2_ps[i][:], w2_sb[:], h1[:, span], start=True, stop=True)
             h2 = work.tile([HIDDEN, width], BF16, name=f"h2{c}")
             score_ps = [product("score_ps", i, 1) for i in range(len(lanes))]
             for i, span in enumerate(spans):
-                relu(h2[:, span], h2_ps[i][:], b2_sb)
+                mlp_relu(h2[:, span], h2_ps[i][:], b2_sb)
                 nc.tensor.matmul(score_ps[i][:], w3_sb[:], h2[:, span], start=True, stop=True)
             for i, span in enumerate(spans):
                 to = score[:, at + span.start : at + span.stop]
                 if narrow:
-                    nc.vector.tensor_scalar_add(to, score_ps[i][:], OUT_BIAS)
-                else:
                     nc.scalar.activation(to, score_ps[i][:], COPY, bias=OUT_BIAS)
+                else:
+                    nc.vector.tensor_scalar_add(to, score_ps[i][:], OUT_BIAS)
             at += width
         nc.sync.dma_start(out, score[:])

import concourse.mybir as mybir

F32, BF16, U16 = mybir.dt.float32, mybir.dt.bfloat16, mybir.dt.uint16
ADD, MAX = mybir.AluOpType.add, mybir.AluOpType.max
RELU = mybir.ActivationFunctionType.Relu
COPY = mybir.ActivationFunctionType.Copy

SIDES, CHANNELS, FEATURES = 2, 256, 512
SLOTS, POSITIONS = 4, 512
HIDDEN = 128
LIST = SIDES * SLOTS * POSITIONS
P = 128
HALVES = CHANNELS // P
BLOCKS = SIDES * HALVES
RUN = POSITIONS // 16
NARROW = 96
CHUNK_LANES = ((160, 128, 128), (NARROW,))
OUT_BIAS = 0.25

FLOPS = 2 * POSITIONS * (SIDES * CHANNELS * HIDDEN + HIDDEN * HIDDEN + HIDDEN)


def tile_halfkpnetwork_kernel(tc, tables, w1, b1, w2, b2, w3, offs, out):
    nc = tc.nc
    table_blocks = tables.rearrange("p (h c) s -> (p h) c s", c=P)

    with (
        tc.tile_pool(name="held", bufs=1) as held,
        tc.tile_pool(name="sums", bufs=2) as sums,
        tc.tile_pool(name="work", bufs=1) as work,
        tc.psum_pool(name="psum", bufs=2) as psum,
    ):
        offsets = held.tile([P, LIST // 16], U16, name="offsets")
        nc.sync.dma_start(offsets[:], offs)
        windows = []
        for b in range(BLOCKS):
            window = held.tile([P, FEATURES], F32, name=f"window{b}")
            nc.sync.dma_start(window[:], table_blocks[b])
            windows.append(window)
        w1_sb = held.tile([P, BLOCKS, HIDDEN], BF16, name="w1_sb")
        nc.sync.dma_start(w1_sb[:], w1.rearrange("(b q) m -> q b m", q=P))
        b1_sb = held.tile([HIDDEN, 1], F32, name="b1_sb")
        nc.sync.dma_start(b1_sb[:], b1)
        w2_sb = held.tile([HIDDEN, HIDDEN], BF16, name="w2_sb")
        nc.sync.dma_start(w2_sb[:], w2)
        b2_sb = held.tile([HIDDEN, 1], F32, name="b2_sb")
        nc.sync.dma_start(b2_sb[:], b2)
        w3_sb = held.tile([HIDDEN, 1], BF16, name="w3_sb")
        nc.sync.dma_start(w3_sb[:], w3)

        acc = [None] * BLOCKS
        for k in range(SLOTS - 1):
            for b in range(BLOCKS):
                run = (b // HALVES) * SLOTS + k
                longer = sums.tile([P, POSITIONS], F32, name=f"acc{b}")
                pieces = 2 if b == 0 and k < 2 else 1
                width = POSITIONS // pieces
                for i in range(pieces):
                    first = run * RUN + i * width // 16
                    picked = windows[b][:].indirect(offsets[:, first : first + width // 16])
                    part = slice(i * width, (i + 1) * width)
                    if k == 0:
                        nc.vector.tensor_copy(longer[:, part], picked)
                    else:
                        nc.vector.tensor_tensor(longer[:, part], picked, acc[b][:, part], ADD)
                acc[b] = longer

        def relu_on_scalar(to, of, bias=None):
            nc.scalar.activation(to, of, RELU, bias=0.0 if bias is None else bias[:])

        def relu_on_vector(to, of, bias):
            nc.vector.tensor_scalar(to, of, bias[:], 0.0, ADD, MAX)

        score = held.tile([1, POSITIONS], F32, name="score")
        at = 0
        for c, lanes in enumerate(CHUNK_LANES):
            narrow = c == len(CHUNK_LANES) - 1
            width = sum(lanes)
            mlp_relu = relu_on_scalar if narrow else relu_on_vector
            spans = [slice(sum(lanes[:i]), sum(lanes[: i + 1])) for i in range(len(lanes))]

            def product(name, i, rows):
                return psum.tile([rows, lanes[i]], F32, name=f"{name}{c}{i}", tag=f"lane{c}{i}")

            h1_ps = [product("h1_ps", i, HIDDEN) for i in range(len(lanes))]
            for b in range(BLOCKS):
                first = (((b // HALVES) * SLOTS + SLOTS - 1) * POSITIONS + at) // 16
                picked = windows[b][:].indirect(offsets[:, first : first + width // 16])
                bag = work.tile([P, width], F32, name=f"bag{c}{b}")
                nc.vector.tensor_tensor(bag[:], picked, acc[b][:, at : at + width], ADD)
                x = work.tile([P, width], BF16, name=f"x{c}{b}")
                if b < BLOCKS - 1 or narrow:
                    relu_on_scalar(x[:], bag[:])
                for i, span in enumerate(spans):
                    if b == BLOCKS - 1 and not narrow:
                        relu_on_scalar(x[:, span], bag[:, span])
                    nc.tensor.matmul(h1_ps[i][:], w1_sb[:, b, :], x[:, span], start=(b == 0), stop=(b == BLOCKS - 1))
            h1 = work.tile([HIDDEN, width], BF16, name=f"h1{c}")
            h2_ps = [product("h2_ps", i, HIDDEN) for i in range(len(lanes))]
            for i, span in enumerate(spans):
                mlp_relu(h1[:, span], h1_ps[i][:], b1_sb)
                nc.tensor.matmul(h2_ps[i][:], w2_sb[:], h1[:, span], start=True, stop=True)
            h2 = work.tile([HIDDEN, width], BF16, name=f"h2{c}")
            score_ps = [product("score_ps", i, 1) for i in range(len(lanes))]
            for i, span in enumerate(spans):
                mlp_relu(h2[:, span], h2_ps[i][:], b2_sb)
                nc.tensor.matmul(score_ps[i][:], w3_sb[:], h2[:, span], start=True, stop=True)
            for i, span in enumerate(spans):
                to = score[:, at + span.start : at + span.stop]
                if narrow:
                    nc.scalar.activation(to, score_ps[i][:], COPY, bias=OUT_BIAS)
                else:
                    nc.vector.tensor_scalar_add(to, score_ps[i][:], OUT_BIAS)
            at += width
        nc.sync.dma_start(out, score[:])
